import numpy as np
import ml_dtypes


def mxq(x, axis, fmt="e4m3"):
    dtype, down = {"e4m3": (ml_dtypes.float8_e4m3fn, 7), "e5m2": (ml_dtypes.float8_e5m2, 14)}[fmt]
    v = np.moveaxis(np.asarray(x, np.float32).astype(ml_dtypes.bfloat16).astype(np.float64), axis, -1)
    blocks = v.reshape(v.shape[:-1] + (-1, 32))
    amax = np.abs(blocks).max(-1, keepdims=True)
    byte = np.maximum(np.where(amax > 0, np.frexp(amax)[1] - 1 + 127, 0) - down, 1)
    scale = np.exp2(byte - 127.0)
    codes = (blocks / scale).astype(np.float32).astype(dtype).astype(np.float64)
    return np.moveaxis((codes * scale).reshape(v.shape), -1, axis)


WIDE = False


def mx_kscale(k):
    if not WIDE:
        return np.ones(k)
    levels = np.array([10, -10, 5, -5, 0])
    a = np.random.permutation(np.resize(levels, k // 512 * 4)).reshape(k // 512, 4)
    idx = np.arange(k)
    return np.exp2(a[idx // 512, idx % 128 // 32])


BF16 = ml_dtypes.bfloat16


def bf(x):
    return np.asarray(x, np.float32).astype(BF16)


def f64(x):
    return np.asarray(x).astype(np.float64)


B, S, IN, OUT = 4, 128, 2048, 2048


def setup_inputs():
    s = mx_kscale(IN)
    w = np.random.standard_normal((OUT, IN + 1))
    w[:, :IN] *= 0.25 / np.sqrt(IN) / s
    w[:, IN] *= 0.5
    return {"x": bf(np.random.standard_normal((B, S, IN)) * s), "weight": bf(w)}


def reference(x, weight):
    w = f64(weight)
    in_features = w.shape[1] - 1
    xf = f64(x).reshape(-1, in_features)
    wm, wb = w[:, :in_features], w[:, in_features]
    xq = mxq(xf, 1, "e4m3")
    wq = mxq(wm, 1, "e4m3")
    lin = (xq @ wq.T) + wb
    ab = (np.abs(xq) @ np.abs(wq).T) + np.abs(wb)
    return 0.5 * (lin + ab)

@@ -1,0 +1,174 @@
+from contextlib import ExitStack
+
+import concourse.mybir as mybir
+from concourse.masks import make_identity
+
+F32 = mybir.dt.float32
+BF16 = mybir.dt.bfloat16
+I32 = mybir.dt.int32
+U8 = mybir.dt.uint8
+FP8X4 = mybir.dt.float8_e4m3fn_x4
+ALU = mybir.AluOpType
+ACT = mybir.ActivationFunctionType
+
+P = 128
+PACK = 4
+K = 2048
+PASSES = K // (P * PACK)
+TOKENS = 512
+OUT = 2048
+BLOCK = 256
+ROW_TILES = BLOCK // P
+X_BLOCKS = TOKENS // BLOCK
+W_BLOCKS = OUT // BLOCK
+BANK = 512
+AHEAD = 4
+FIRST_NEEDS = 3
+NO_SIGNS = 0x7FFF7FFF
+
+FLOPS = 2 * 2 * TOKENS * K * OUT
+
+
+def tile_skanlinear_kernel(tc, x, weight, out):
+    nc = tc.nc
+    x2 = x.flatten_outer_dims()
+    out_tiles = out.rearrange("(t p) o -> p t o", p=P)
+
+    with ExitStack() as stack:
+        stack.enter_context(tc.manual_schedule())
+        const = stack.enter_context(tc.tile_pool(name="const", bufs=1))
+        raw_pool = stack.enter_context(tc.tile_pool(name="raw", bufs=8))
+        grouped_pool = stack.enter_context(tc.tile_pool(name="grouped", bufs=3))
+        plain_pool = stack.enter_context(tc.tile_pool(name="plain", bufs=2))
+        keep = stack.enter_context(tc.tile_pool(name="keep", bufs=1))
+        y_pool = stack.enter_context(tc.tile_pool(name="y", bufs=4))
+        flip_psum = stack.enter_context(tc.psum_pool(name="flip", bufs=4))
+        acc_psum = stack.enter_context(tc.psum_pool(name="acc", bufs=4))
+
+        ident_f32 = const.tile([P, P], F32)
+        make_identity(nc, ident_f32[:])
+        ident_bf16 = const.tile([P, P], BF16)
+        make_identity(nc, ident_bf16[:])
+
+        sources = [("x0", x2[0:BLOCK, :]), ("w0", weight[0:BLOCK, 0:K]), ("x1", x2[BLOCK : 2 * BLOCK, :])]
+        for b in range(1, W_BLOCKS):
+            sources.append(("w%d" % b, weight[b * BLOCK : (b + 1) * BLOCK, 0:K]))
+
+        def load(rows):
+            raw = raw_pool.tile([P, ROW_TILES, K], BF16)
+            for r in range(ROW_TILES):
+                nc.sync.dma_start(out=raw[:, r, :], in_=rows[r * P : (r + 1) * P, :])
+            return raw
+
+        def load_bias():
+            bias_col = const.tile([P, OUT // P], BF16)
+            with nc.allow_non_contiguous_dma(reason="the bias is a column of weight"):
+                nc.sync.dma_start(
+                    out=bias_col[:].unsqueeze(2), in_=weight[:, K : K + 1].rearrange("(t p) one -> p t one", p=P)
+                )
+            return bias_col
+
+        def spread_bias(bias_col):
+            bias_rows = const.tile([P, OUT], F32)
+            for c in range(OUT // BANK):
+                bank = flip_psum.tile([P, BANK], F32, tag="bank")
+                for t in range(BANK // P):
+                    nc.tensor.matmul(
+                        out=bank[:, t * P : (t + 1) * P],
+                        lhsT=bias_col[:, c * (BANK // P) + t : c * (BANK // P) + t + 1].to_broadcast([P, P]),
+                        rhs=ident_bf16[:],
+                        start=True,
+                        stop=True,
+                    )
+                nc.scalar.activation(out=bias_rows[:, c * BANK : (c + 1) * BANK], in_=bank[:], func=ACT.Relu)
+            return bias_rows
+
+        def transpose(raw):
+            words = raw[:].bitcast(F32)
+            grouped = grouped_pool.tile([P, PASSES, BLOCK, PACK], BF16, align_bytes=64)
+            grouped_words = grouped[:].bitcast(F32)
+            for g in range(PASSES):
+                bank = flip_psum.tile([P, 2, BLOCK], F32, tag="bank")
+                for u in range(2):
+                    first = (2 * g + u) * P
+                    for r in range(ROW_TILES):
+                        nc.tensor.transpose(
+                            bank[:, u, r * P : (r + 1) * P], words[:, r, first : first + P], ident_f32[:]
+                        )
+                nc.scalar.copy(out=grouped_words[:, g, :, :], in_=bank[:].rearrange("p u o -> p o u"))
+            return grouped
+
+        def quantise_one(name, values):
+            codes = keep.tile([P, PASSES, BLOCK], I32, name="codes_" + name, align_bytes=64)
+            scales = keep.tile([P, PASSES, BLOCK], U8, name="scales_" + name, align_bytes=64)
+            nc.vector.quantize_mx(
+                out=codes[:].rearrange("p g o -> p (g o)").bitcast(FP8X4),
+                scales=scales[:].rearrange("p g o -> p (g o)"),
+                in_=values[:].rearrange("p g o t -> p (g o t)"),
+            )
+            return (codes, scales)
+
+        def quantise(label, grouped):
+            plain = plain_pool.tile([P, PASSES, BLOCK, PACK], BF16, align_bytes=64)
+            nc.vector.tensor_scalar(
+                out=plain[:].bitcast(I32),
+                in0=grouped[:].bitcast(I32),
+                scalar1=NO_SIGNS,
+                scalar2=None,
+                op0=ALU.bitwise_and,
+            )
+            return (quantise_one(label, grouped), quantise_one("abs_" + label, plain))
+
+        def multiply(b, x_ready, w_ready, bias_rows):
+            cols = slice(b * BLOCK, (b + 1) * BLOCK)
+            for pair in range(X_BLOCKS):
+                acc = acc_psum.tile([P, ROW_TILES, BLOCK], F32)
+                for half in range(ROW_TILES):
+                    tokens = slice(half * P, (half + 1) * P)
+                    for kind in range(2):
+                        x_codes, x_scales = x_ready[pair][kind]
+                        w_codes, w_scales = w_ready[kind]
+                        for g in range(PASSES):
+                            nc.tensor.matmul_mx(
+                                out=acc[:, half, :],
+                                lhsT=x_codes[:, g, tokens].bitcast(FP8X4),
+                                lhsT_scale=x_scales[:, g, tokens],
+                                rhs=w_codes[:, g, :].bitcast(FP8X4),
+                                rhs_scale=w_scales[:, g, :],
+                                start=(kind == 0 and g == 0),
+                                stop=(kind == 1 and g == PASSES - 1),
+                            )
+                y = y_pool.tile([P, ROW_TILES, BLOCK], F32)
+                nc.vector.scalar_tensor_tensor(
+                    out=y[:],
+                    in0=acc[:],
+                    scalar=0.5,
+                    in1=bias_rows[:, cols].unsqueeze(1).to_broadcast([P, ROW_TILES, BLOCK]),
+                    op0=ALU.mult,
+                    op1=ALU.add,
+                )
+                nc.sync.dma_start(
+                    out=out_tiles[:, pair * ROW_TILES : (pair + 1) * ROW_TILES, cols], in_=y[:]
+                )
+
+        raws = []
+        bias_col = None
+        for i in range(len(sources)):
+            raws.append(load(sources[i][1]))
+            if i == FIRST_NEEDS - 1:
+                bias_col = load_bias()
+
+        grouped_tiles = {}
+        ready = {}
+        bias_rows = None
+        for step in range(W_BLOCKS + AHEAD):
+            if step < len(sources):
+                grouped_tiles[step] = transpose(raws[step])
+            if step == FIRST_NEEDS - 1:
+                bias_rows = spread_bias(bias_col)
+            if 1 <= step <= len(sources):
+                label = sources[step - 1][0]
+                ready[label] = quantise(label, grouped_tiles[step - 1])
+            if step >= AHEAD:
+                b = step - AHEAD
+                multiply(b, [ready["x0"], ready["x1"]], ready["w%d" % b], bias_rows)

@@ -21,9 +21,8 @@ BLOCK = 256
 ROW_TILES = BLOCK // P
 X_BLOCKS = TOKENS // BLOCK
 W_BLOCKS = OUT // BLOCK
-BANK = 512
+ROW_PITCH = K + 32
 AHEAD = 4
-FIRST_NEEDS = 3
 NO_SIGNS = 0x7FFF7FFF
 
 FLOPS = 2 * 2 * TOKENS * K * OUT
@@ -43,48 +42,40 @@ def tile_skanlinear_kernel(tc, x, weight, out):
         keep = stack.enter_context(tc.tile_pool(name="keep", bufs=1))
         y_pool = stack.enter_context(tc.tile_pool(name="y", bufs=4))
         flip_psum = stack.enter_context(tc.psum_pool(name="flip", bufs=4))
-        acc_psum = stack.enter_context(tc.psum_pool(name="acc", bufs=4))
+        acc_psum = stack.enter_context(tc.psum_pool(name="acc", bufs=3))
+        bias_psum = stack.enter_context(tc.psum_pool(name="bias", bufs=1))
 
         ident_f32 = const.tile([P, P], F32)
         make_identity(nc, ident_f32[:])
         ident_bf16 = const.tile([P, P], BF16)
         make_identity(nc, ident_bf16[:])
 
-        sources = [("x0", x2[0:BLOCK, :]), ("w0", weight[0:BLOCK, 0:K]), ("x1", x2[BLOCK : 2 * BLOCK, :])]
+        bias_rows = const.tile([P, OUT], F32)
+
+        sources = [("x0", x2[0:BLOCK, :], None), ("w0", weight[0:BLOCK, :], 0), ("x1", x2[BLOCK : 2 * BLOCK, :], None)]
         for b in range(1, W_BLOCKS):
-            sources.append(("w%d" % b, weight[b * BLOCK : (b + 1) * BLOCK, 0:K]))
+            sources.append(("w%d" % b, weight[b * BLOCK : (b + 1) * BLOCK, :], b))
 
         def load(rows):
-            raw = raw_pool.tile([P, ROW_TILES, K], BF16)
+            raw = raw_pool.tile([P, ROW_TILES, ROW_PITCH], BF16)
             for r in range(ROW_TILES):
-                nc.sync.dma_start(out=raw[:, r, :], in_=rows[r * P : (r + 1) * P, :])
+                nc.sync.dma_start(out=raw[:, r, 0 : rows.shape[1]], in_=rows[r * P : (r + 1) * P, :])
             return raw
 
-        def load_bias():
-            bias_col = const.tile([P, OUT // P], BF16)
-            with nc.allow_non_contiguous_dma(reason="the bias is a column of weight"):
-                nc.sync.dma_start(
-                    out=bias_col[:].unsqueeze(2), in_=weight[:, K : K + 1].rearrange("(t p) one -> p t one", p=P)
+        def spread_bias(b, raw):
+            bank = bias_psum.tile([P, BLOCK], F32)
+            for r in range(ROW_TILES):
+                nc.tensor.matmul(
+                    out=bank[:, r * P : (r + 1) * P],
+                    lhsT=raw[:, r, K : K + 1].to_broadcast([P, P]),
+                    rhs=ident_bf16[:],
+                    start=True,
+                    stop=True,
                 )
-            return bias_col
-
-        def spread_bias(bias_col):
-            bias_rows = const.tile([P, OUT], F32)
-            for c in range(OUT // BANK):
-                bank = flip_psum.tile([P, BANK], F32, tag="bank")
-                for t in range(BANK // P):
-                    nc.tensor.matmul(
-                        out=bank[:, t * P : (t + 1) * P],
-                        lhsT=bias_col[:, c * (BANK // P) + t : c * (BANK // P) + t + 1].to_broadcast([P, P]),
-                        rhs=ident_bf16[:],
-                        start=True,
-                        stop=True,
-                    )
-                nc.scalar.activation(out=bias_rows[:, c * BANK : (c + 1) * BANK], in_=bank[:], func=ACT.Relu)
-            return bias_rows
+            nc.scalar.activation(out=bias_rows[:, b * BLOCK : (b + 1) * BLOCK], in_=bank[:], func=ACT.Relu)
 
         def transpose(raw):
-            words = raw[:].bitcast(F32)
+            words = raw[:, :, 0:K].bitcast(F32)
             grouped = grouped_pool.tile([P, PASSES, BLOCK, PACK], BF16, align_bytes=64)
             grouped_words = grouped[:].bitcast(F32)
             for g in range(PASSES):
@@ -119,7 +110,7 @@ def tile_skanlinear_kernel(tc, x, weight, out):
             )
             return (quantise_one(label, grouped), quantise_one("abs_" + label, plain))
 
-        def multiply(b, x_ready, w_ready, bias_rows):
+        def multiply(b, x_ready, w_ready):
             cols = slice(b * BLOCK, (b + 1) * BLOCK)
             for pair in range(X_BLOCKS):
                 acc = acc_psum.tile([P, ROW_TILES, BLOCK], F32)
@@ -152,23 +143,19 @@ def tile_skanlinear_kernel(tc, x, weight, out):
                 )
 
         raws = []
-        bias_col = None
-        for i in range(len(sources)):
-            raws.append(load(sources[i][1]))
-            if i == FIRST_NEEDS - 1:
-                bias_col = load_bias()
+        for source in sources:
+            raws.append(load(source[1]))
 
         grouped_tiles = {}
         ready = {}
-        bias_rows = None
         for step in range(W_BLOCKS + AHEAD):
             if step < len(sources):
                 grouped_tiles[step] = transpose(raws[step])
-            if step == FIRST_NEEDS - 1:
-                bias_rows = spread_bias(bias_col)
+                if sources[step][2] is not None:
+                    spread_bias(sources[step][2], raws[step])
             if 1 <= step <= len(sources):
                 label = sources[step - 1][0]
                 ready[label] = quantise(label, grouped_tiles[step - 1])
             if step >= AHEAD:
                 b = step - AHEAD
-                multiply(b, [ready["x0"], ready["x1"]], ready["w%d" % b], bias_rows)
+                multiply(b, [ready["x0"], ready["x1"]], ready["w%d" % b])

@@ -34,7 +34,6 @@ def tile_skanlinear_kernel(tc, x, weight, out):
     out_tiles = out.rearrange("(t p) o -> p t o", p=P)
 
     with ExitStack() as stack:
-        stack.enter_context(tc.manual_schedule())
         const = stack.enter_context(tc.tile_pool(name="const", bufs=1))
         raw_pool = stack.enter_context(tc.tile_pool(name="raw", bufs=8))
         grouped_pool = stack.enter_context(tc.tile_pool(name="grouped", bufs=3))

from contextlib import ExitStack

import concourse.mybir as mybir
from concourse.masks import make_identity

F32 = mybir.dt.float32
BF16 = mybir.dt.bfloat16
I32 = mybir.dt.int32
U8 = mybir.dt.uint8
FP8X4 = mybir.dt.float8_e4m3fn_x4
ALU = mybir.AluOpType
ACT = mybir.ActivationFunctionType

P = 128
PACK = 4
K = 2048
PASSES = K // (P * PACK)
TOKENS = 512
OUT = 2048
BLOCK = 256
ROW_TILES = BLOCK // P
X_BLOCKS = TOKENS // BLOCK
W_BLOCKS = OUT // BLOCK
ROW_PITCH = K + 32
AHEAD = 4
NO_SIGNS = 0x7FFF7FFF

FLOPS = 2 * 2 * TOKENS * K * OUT


def tile_skanlinear_kernel(tc, x, weight, out):
    nc = tc.nc
    x2 = x.flatten_outer_dims()
    out_tiles = out.rearrange("(t p) o -> p t o", p=P)

    with ExitStack() as stack:
        const = stack.enter_context(tc.tile_pool(name="const", bufs=1))
        raw_pool = stack.enter_context(tc.tile_pool(name="raw", bufs=8))
        grouped_pool = stack.enter_context(tc.tile_pool(name="grouped", bufs=3))
        plain_pool = stack.enter_context(tc.tile_pool(name="plain", bufs=2))
        keep = stack.enter_context(tc.tile_pool(name="keep", bufs=1))
        y_pool = stack.enter_context(tc.tile_pool(name="y", bufs=4))
        flip_psum = stack.enter_context(tc.psum_pool(name="flip", bufs=4))
        acc_psum = stack.enter_context(tc.psum_pool(name="acc", bufs=3))
        bias_psum = stack.enter_context(tc.psum_pool(name="bias", bufs=1))

        ident_f32 = const.tile([P, P], F32)
        make_identity(nc, ident_f32[:])
        ident_bf16 = const.tile([P, P], BF16)
        make_identity(nc, ident_bf16[:])

        bias_rows = const.tile([P, OUT], F32)

        sources = [("x0", x2[0:BLOCK, :], None), ("w0", weight[0:BLOCK, :], 0), ("x1", x2[BLOCK : 2 * BLOCK, :], None)]
        for b in range(1, W_BLOCKS):
            sources.append(("w%d" % b, weight[b * BLOCK : (b + 1) * BLOCK, :], b))

        def load(rows):
            raw = raw_pool.tile([P, ROW_TILES, ROW_PITCH], BF16)
            for r in range(ROW_TILES):
                nc.sync.dma_start(out=raw[:, r, 0 : rows.shape[1]], in_=rows[r * P : (r + 1) * P, :])
            return raw

        def spread_bias(b, raw):
            bank = bias_psum.tile([P, BLOCK], F32)
            for r in range(ROW_TILES):
                nc.tensor.matmul(
                    out=bank[:, r * P : (r + 1) * P],
                    lhsT=raw[:, r, K : K + 1].to_broadcast([P, P]),
                    rhs=ident_bf16[:],
                    start=True,
                    stop=True,
                )
            nc.scalar.activation(out=bias_rows[:, b * BLOCK : (b + 1) * BLOCK], in_=bank[:], func=ACT.Relu)

        def transpose(raw):
            words = raw[:, :, 0:K].bitcast(F32)
            grouped = grouped_pool.tile([P, PASSES, BLOCK, PACK], BF16, align_bytes=64)
            grouped_words = grouped[:].bitcast(F32)
            for g in range(PASSES):
                bank = flip_psum.tile([P, 2, BLOCK], F32, tag="bank")
                for u in range(2):
                    first = (2 * g + u) * P
                    for r in range(ROW_TILES):
                        nc.tensor.transpose(
                            bank[:, u, r * P : (r + 1) * P], words[:, r, first : first + P], ident_f32[:]
                        )
                nc.scalar.copy(out=grouped_words[:, g, :, :], in_=bank[:].rearrange("p u o -> p o u"))
            return grouped

        def quantise_one(name, values):
            codes = keep.tile([P, PASSES, BLOCK], I32, name="codes_" + name, align_bytes=64)
            scales = keep.tile([P, PASSES, BLOCK], U8, name="scales_" + name, align_bytes=64)
            nc.vector.quantize_mx(
                out=codes[:].rearrange("p g o -> p (g o)").bitcast(FP8X4),
                scales=scales[:].rearrange("p g o -> p (g o)"),
                in_=values[:].rearrange("p g o t -> p (g o t)"),
            )
            return (codes, scales)

        def quantise(label, grouped):
            plain = plain_pool.tile([P, PASSES, BLOCK, PACK], BF16, align_bytes=64)
            nc.vector.tensor_scalar(
                out=plain[:].bitcast(I32),
                in0=grouped[:].bitcast(I32),
                scalar1=NO_SIGNS,
                scalar2=None,
                op0=ALU.bitwise_and,
            )
            return (quantise_one(label, grouped), quantise_one("abs_" + label, plain))

        def multiply(b, x_ready, w_ready):
            cols = slice(b * BLOCK, (b + 1) * BLOCK)
            for pair in range(X_BLOCKS):
                acc = acc_psum.tile([P, ROW_TILES, BLOCK], F32)
                for half in range(ROW_TILES):
                    tokens = slice(half * P, (half + 1) * P)
                    for kind in range(2):
                        x_codes, x_scales = x_ready[pair][kind]
                        w_codes, w_scales = w_ready[kind]
                        for g in range(PASSES):
                            nc.tensor.matmul_mx(
                                out=acc[:, half, :],
                                lhsT=x_codes[:, g, tokens].bitcast(FP8X4),
                                lhsT_scale=x_scales[:, g, tokens],
                                rhs=w_codes[:, g, :].bitcast(FP8X4),
                                rhs_scale=w_scales[:, g, :],
                                start=(kind == 0 and g == 0),
                                stop=(kind == 1 and g == PASSES - 1),
                            )
                y = y_pool.tile([P, ROW_TILES, BLOCK], F32)
                nc.vector.scalar_tensor_tensor(
                    out=y[:],
                    in0=acc[:],
                    scalar=0.5,
                    in1=bias_rows[:, cols].unsqueeze(1).to_broadcast([P, ROW_TILES, BLOCK]),
                    op0=ALU.mult,
                    op1=ALU.add,
                )
                nc.sync.dma_start(
                    out=out_tiles[:, pair * ROW_TILES : (pair + 1) * ROW_TILES, cols], in_=y[:]
                )

        raws = []
        for source in sources:
            raws.append(load(source[1]))

        grouped_tiles = {}
        ready = {}
        for step in range(W_BLOCKS + AHEAD):
            if step < len(sources):
                grouped_tiles[step] = transpose(raws[step])
                if sources[step][2] is not None:
                    spread_bias(sources[step][2], raws[step])
            if 1 <= step <= len(sources):
                label = sources[step - 1][0]
                ready[label] = quantise(label, grouped_tiles[step - 1])
            if step >= AHEAD:
                b = step - AHEAD
                multiply(b, [ready["x0"], ready["x1"]], ready["w%d" % b])
